import numpy as np
import ml_dtypes


def mxq(x, axis, fmt="e4m3"):
    dtype, down = {"e4m3": (ml_dtypes.float8_e4m3fn, 7), "e5m2": (ml_dtypes.float8_e5m2, 14)}[fmt]
    v = np.moveaxis(np.asarray(x, np.float32).astype(ml_dtypes.bfloat16).astype(np.float64), axis, -1)
    blocks = v.reshape(v.shape[:-1] + (-1, 32))
    amax = np.abs(blocks).max(-1, keepdims=True)
    byte = np.maximum(np.where(amax > 0, np.frexp(amax)[1] - 1 + 127, 0) - down, 1)
    scale = np.exp2(byte - 127.0)
    codes = (blocks / scale).astype(np.float32).astype(dtype).astype(np.float64)
    return np.moveaxis((codes * scale).reshape(v.shape), -1, axis)


WIDE = False


def mx_kscale(k):
    if not WIDE:
        return np.ones(k)
    levels = np.array([10, -10, 5, -5, 0])
    a = np.random.permutation(np.resize(levels, k // 512 * 4)).reshape(k // 512, 4)
    idx = np.arange(k)
    return np.exp2(a[idx // 512, idx % 128 // 32])


BF16 = ml_dtypes.bfloat16


def bf(x):
    return np.asarray(x, np.float32).astype(BF16)


def f64(x):
    return np.asarray(x).astype(np.float64)


B, V, S, N = 4, 1024, 1024, 1024


def setup_inputs():
    s = mx_kscale(V)
    r = s / s.max()
    d = np.random.standard_normal((B, V, S)) * (0.5 + np.random.random_sample((B, 1, S)))
    d = np.copysign(np.sqrt(d * d - np.log(r)[None, :, None]), d)
    return {"fi_v": bf(np.random.standard_normal((B, V, N)) * 0.4 * np.sqrt(V) / r[None, :, None]), "d_av": bf(d)}


def reference(fi_v, d_av):
    w = np.exp(-np.square(f64(d_av)))
    hi = (mxq(w, 1, "e4m3").transpose(0, 2, 1) @ mxq(f64(fi_v), 1, "e4m3")) / fi_v.shape[1]
    wbar = np.mean(w, axis=1)
    out = wbar[:, :, None] * hi
    return out.reshape(out.shape[0], -1)

@@ -1,0 +1,197 @@
+from contextlib import ExitStack
+
+import concourse.mybir as mybir
+from concourse.masks import make_identity
+
+FLOPS = 2 * 4 * 1024 * 1024 * 1024
+
+F32 = mybir.dt.float32
+BF16 = mybir.dt.bfloat16
+U32 = mybir.dt.uint32
+U8 = mybir.dt.uint8
+FP8X4 = mybir.dt.float8_e4m3fn_x4
+ACT = mybir.ActivationFunctionType
+ALU = mybir.AluOpType
+AX = mybir.AxisListType
+
+P = 128
+PACK = 4
+GRAPHS = 4
+V = 1024
+S = 1024
+N = 1024
+PASSES = V // (P * PACK)
+PLANES = PASSES * PACK
+WS = 256
+UNITS = S // WS
+MB = WS // P
+NT = 512
+NH = N // NT
+ACT_EXITS = [2, 2, 2, 1, 1, 2, 1, 1, 1, 2, 1, 1, 0, 0, 1, 2]
+
+
+def tile_garnetlayer_t_kernel(tc, fi_v, d_av, out):
+    nc = tc.nc
+    d_view = d_av.rearrange("b (h p j) s -> b h p j s", h=PASSES, p=P, j=PACK)
+    f_view = fi_v.rearrange("b (h p j) n -> b h p j n", h=PASSES, p=P, j=PACK)
+    o_view = out.rearrange("b (m p n) -> b m p n", m=S // P, p=P, n=N)
+
+    with ExitStack() as ctx:
+        const = ctx.enter_context(tc.tile_pool(name="const", bufs=1))
+        rawd = ctx.enter_context(tc.tile_pool(name="rawd", bufs=GRAPHS))
+        rawf = ctx.enter_context(tc.tile_pool(name="rawf", bufs=GRAPHS * PASSES))
+        wpool = ctx.enter_context(tc.tile_pool(name="wpool", bufs=3))
+        gpool = ctx.enter_context(tc.tile_pool(name="gpool", bufs=2))
+        wq = ctx.enter_context(tc.tile_pool(name="wq", bufs=3))
+        fq = ctx.enter_context(tc.tile_pool(name="fq", bufs=2))
+        small = ctx.enter_context(tc.tile_pool(name="small", bufs=4))
+        outp = ctx.enter_context(tc.tile_pool(name="outp", bufs=6))
+        ps_sum = ctx.enter_context(tc.psum_pool(name="ps_sum", bufs=2))
+        ps_acc = ctx.enter_context(tc.psum_pool(name="ps_acc", bufs=6))
+
+        ident = const.tile([P, P], F32)
+        make_identity(nc, ident[:])
+
+        d_raw = {}
+        f_raw = {}
+        f_codes = {}
+        f_scales = {}
+
+        def load_d(b, cuts):
+            d_raw[b] = rawd.tile([P, PASSES, PACK, S], BF16, name="d_raw")
+            for lo, hi in cuts:
+                for h in range(PASSES):
+                    nc.sync.dma_start(out=d_raw[b][:, h, :, lo:hi], in_=d_view[b, h][:, :, lo:hi])
+
+        def load_f(b, h):
+            f_raw[(b, h)] = rawf.tile([P, PACK, N], BF16, name="f_raw")
+            nc.sync.dma_start(out=f_raw[(b, h)][:], in_=f_view[b, h])
+
+        def f_tiles(b):
+            f_codes[b] = fq.tile([P, PASSES, N], U32, name="f_codes", align_bytes=64)
+            f_scales[b] = fq.tile([P, PASSES, N], U8, name="f_scales", align_bytes=64)
+
+        def f_regroup(b, piece):
+            h, nh = divmod(piece, NH)
+            fg = gpool.tile([P, NT, PACK], BF16, name="fg", align_bytes=64)
+            nc.vector.tensor_copy(
+                out=fg[:].rearrange("p (c i) t -> p c t i", i=4),
+                in_=f_raw[(b, h)][:, :, nh * NT:(nh + 1) * NT].rearrange("p t (c i) -> p c t i", i=4),
+            )
+            return fg
+
+        def f_quant(b, piece, fg):
+            h, nh = divmod(piece, NH)
+            cols = slice(nh * NT, (nh + 1) * NT)
+            nc.vector.quantize_mx(
+                out=f_codes[b][:, h, cols].bitcast(FP8X4),
+                scales=f_scales[b][:, h, cols],
+                in_=fg[:].rearrange("p n t -> p (n t)"),
+            )
+
+        def w_exp(g):
+            b, u = divmod(g, UNITS)
+            w32 = wpool.tile([P, PLANES, WS], F32, name="w32")
+            src = d_raw[b][:].rearrange("p h j s -> p (h j) s")[:, :, u * WS:(u + 1) * WS]
+            nc.scalar.activation(out=w32[:], in_=src, func=ACT.Square)
+            nc.scalar.activation(out=w32[:], in_=w32[:], func=ACT.Exp, scale=-1.0)
+            return w32
+
+        def w_sum_pe(w32):
+            pw = ps_sum.tile([P, MB, P], F32, name="pw")
+            for mm in range(MB):
+                for k in range(PLANES):
+                    nc.tensor.matmul(
+                        out=pw[:, mm, :],
+                        lhsT=w32[:, k, mm * P:(mm + 1) * P],
+                        rhs=ident[:],
+                        is_transpose=True,
+                        start=(k == 0),
+                        stop=(k == PLANES - 1),
+                    )
+            return pw
+
+        def w_cast(w32):
+            wg = gpool.tile([P, PASSES, WS, PACK], BF16, name="wg", align_bytes=64)
+            nc.vector.tensor_copy(
+                out=wg[:].rearrange("p h (c i) j -> p h c j i", i=4),
+                in_=w32[:].rearrange("p (h j) (c i) -> p h c j i", h=PASSES, i=4),
+            )
+            return wg
+
+        def w_quant(wg):
+            wc = wq.tile([P, PASSES * WS], U32, name="wc", align_bytes=64)
+            wl = wq.tile([P, PASSES * WS], U8, name="wl", align_bytes=64)
+            nc.vector.quantize_mx(
+                out=wc[:].bitcast(FP8X4), scales=wl[:], in_=wg[:].rearrange("p h s j -> p (h s j)")
+            )
+            return wc, wl
+
+        def w_bar(pw):
+            wsum = small.tile([P, MB], F32, name="wsum")
+            nc.vector.tensor_reduce(out=wsum[:], in_=pw[:], axis=AX.X, op=ALU.add)
+            wbar = small.tile([P, MB], F32, name="wbar")
+            nc.vector.tensor_scalar(out=wbar[:], in0=wsum[:], scalar1=2.0 ** -20, scalar2=None, op0=ALU.mult)
+            return wbar
+
+        def multiply(g, wc, wl, wbar):
+            b, u = divmod(g, UNITS)
+            for mm in range(MB):
+                o = outp.tile([P, N], F32, name="o")
+                for nh in range(NH):
+                    cols = slice(nh * NT, (nh + 1) * NT)
+                    acc = ps_acc.tile([P, NT], F32, name="acc")
+                    for h in range(PASSES):
+                        wcols = slice(h * WS + mm * P, h * WS + (mm + 1) * P)
+                        nc.tensor.matmul_mx(
+                            out=acc[:],
+                            lhsT=wc[:, wcols].bitcast(FP8X4),
+                            lhsT_scale=wl[:, wcols],
+                            rhs=f_codes[b][:, h, cols].bitcast(FP8X4),
+                            rhs_scale=f_scales[b][:, h, cols],
+                            start=(h == 0),
+                            stop=(h == PASSES - 1),
+                        )
+                    if mm * NH + nh < MB * NH - ACT_EXITS[g]:
+                        nc.vector.tensor_scalar(
+                            out=o[:, cols], in0=acc[:], scalar1=wbar[:, mm:mm + 1], scalar2=None, op0=ALU.mult
+                        )
+                    else:
+                        nc.scalar.activation(out=o[:, cols], in_=acc[:], func=ACT.Copy, scale=wbar[:, mm:mm + 1])
+                nc.sync.dma_start(out=o_view[b, u * MB + mm], in_=o[:])
+
+        load_d(0, [(0, WS), (WS, 2 * WS)])
+        load_f(0, 0)
+        for h in range(PASSES):
+            nc.sync.dma_start(out=d_raw[0][:, h, :, 2 * WS:S], in_=d_view[0, h][:, :, 2 * WS:S])
+        load_f(0, 1)
+        for b in range(1, GRAPHS):
+            load_f(b, 0)
+            load_f(b, 1)
+            load_d(b, [(0, S)])
+
+        total = GRAPHS * UNITS
+        w32s = {0: w_exp(0)}
+        f_tiles(0)
+        fgs = {}
+        for piece in range(PASSES * NH):
+            fgs[piece] = f_regroup(0, piece)
+            if piece > 0:
+                f_quant(0, piece - 1, fgs[piece - 1])
+        f_quant(0, PASSES * NH - 1, fgs[PASSES * NH - 1])
+        for g in range(total):
+            b, u = divmod(g, UNITS)
+            if g + 1 < total:
+                w32s[g + 1] = w_exp(g + 1)
+            pw = w_sum_pe(w32s[g])
+            wg = w_cast(w32s[g])
+            fg = None
+            if b + 1 < GRAPHS:
+                if u == 0:
+                    f_tiles(b + 1)
+                fg = f_regroup(b + 1, u)
+            wc, wl = w_quant(wg)
+            if fg is not None:
+                f_quant(b + 1, u, fg)
+            wbar = w_bar(pw)
+            multiply(g, wc, wl, wbar)

@@ -22,12 +22,11 @@ S = 1024
 N = 1024
 PASSES = V // (P * PACK)
 PLANES = PASSES * PACK
-WS = 256
-UNITS = S // WS
-MB = WS // P
 NT = 512
 NH = N // NT
-ACT_EXITS = [2, 2, 2, 1, 1, 2, 1, 1, 1, 2, 1, 1, 0, 0, 1, 2]
+PIECES = PASSES * NH
+WIDTHS = [256] * 15 + [128, 128]
+ACT_EXITS = [3, 3, 2, 1, 1, 2, 1, 1, 1, 2, 1, 1, 1, 0, 3, 2, 0]
 
 
 def tile_garnetlayer_t_kernel(tc, fi_v, d_av, out):
@@ -35,6 +34,13 @@ def tile_garnetlayer_t_kernel(tc, fi_v, d_av, out):
     d_view = d_av.rearrange("b (h p j) s -> b h p j s", h=PASSES, p=P, j=PACK)
     f_view = fi_v.rearrange("b (h p j) n -> b h p j n", h=PASSES, p=P, j=PACK)
     o_view = out.rearrange("b (m p n) -> b m p n", m=S // P, p=P, n=N)
+
+    units = []
+    start = 0
+    for width in WIDTHS:
+        units.append((start // S, start % S, width))
+        start += width
+    total = len(units)
 
     with ExitStack() as ctx:
         const = ctx.enter_context(tc.tile_pool(name="const", bufs=1))
@@ -48,6 +54,7 @@ def tile_garnetlayer_t_kernel(tc, fi_v, d_av, out):
         outp = ctx.enter_context(tc.tile_pool(name="outp", bufs=6))
         ps_sum = ctx.enter_context(tc.psum_pool(name="ps_sum", bufs=2))
         ps_acc = ctx.enter_context(tc.psum_pool(name="ps_acc", bufs=6))
+        ctx.enter_context(tc.manual_schedule())
 
         ident = const.tile([P, P], F32)
         make_identity(nc, ident[:])
@@ -56,22 +63,28 @@ def tile_garnetlayer_t_kernel(tc, fi_v, d_av, out):
         f_raw = {}
         f_codes = {}
         f_scales = {}
+        w32s = {}
+        sums = {}
+        codes = {}
+        bars = {}
+        accs = {}
+        outs = {}
 
-        def load_d(b, cuts):
-            d_raw[b] = rawd.tile([P, PASSES, PACK, S], BF16, name="d_raw")
-            for lo, hi in cuts:
-                for h in range(PASSES):
-                    nc.sync.dma_start(out=d_raw[b][:, h, :, lo:hi], in_=d_view[b, h][:, :, lo:hi])
+        def load_d(b, lo, hi):
+            if b not in d_raw:
+                d_raw[b] = rawd.tile([P, PASSES, PACK, S], BF16, name="d_raw")
+            for h in range(PASSES):
+                nc.sync.dma_start(out=d_raw[b][:, h, :, lo:hi], in_=d_view[b, h][:, :, lo:hi])
 
-        def load_f(b, h):
-            f_raw[(b, h)] = rawf.tile([P, PACK, N], BF16, name="f_raw")
-            nc.sync.dma_start(out=f_raw[(b, h)][:], in_=f_view[b, h])
-
-        def f_tiles(b):
-            f_codes[b] = fq.tile([P, PASSES, N], U32, name="f_codes", align_bytes=64)
-            f_scales[b] = fq.tile([P, PASSES, N], U8, name="f_scales", align_bytes=64)
+        def load_f(b, h, lo, hi):
+            if (b, h) not in f_raw:
+                f_raw[(b, h)] = rawf.tile([P, PACK, N], BF16, name="f_raw")
+            nc.sync.dma_start(out=f_raw[(b, h)][:, :, lo:hi], in_=f_view[b, h][:, :, lo:hi])
 
         def f_regroup(b, piece):
+            if b not in f_codes:
+                f_codes[b] = fq.tile([P, PASSES, N], U32, name="f_codes", align_bytes=64)
+                f_scales[b] = fq.tile([P, PASSES, N], U8, name="f_scales", align_bytes=64)
             h, nh = divmod(piece, NH)
             fg = gpool.tile([P, NT, PACK], BF16, name="fg", align_bytes=64)
             nc.vector.tensor_copy(
@@ -90,59 +103,63 @@ def tile_garnetlayer_t_kernel(tc, fi_v, d_av, out):
             )
 
         def w_exp(g):
-            b, u = divmod(g, UNITS)
-            w32 = wpool.tile([P, PLANES, WS], F32, name="w32")
-            src = d_raw[b][:].rearrange("p h j s -> p (h j) s")[:, :, u * WS:(u + 1) * WS]
+            b, s0, width = units[g]
+            w32 = wpool.tile([P, PLANES, width], F32, name="w32")
+            src = d_raw[b][:].rearrange("p h j s -> p (h j) s")[:, :, s0:s0 + width]
             nc.scalar.activation(out=w32[:], in_=src, func=ACT.Square)
             nc.scalar.activation(out=w32[:], in_=w32[:], func=ACT.Exp, scale=-1.0)
-            return w32
+            w32s[g] = w32
 
-        def w_sum_pe(w32):
-            pw = ps_sum.tile([P, MB, P], F32, name="pw")
-            for mm in range(MB):
+        def w_sum_pe(g):
+            blocks = units[g][2] // P
+            pw = ps_sum.tile([P, blocks, P], F32, name="pw")
+            for mm in range(blocks):
                 for k in range(PLANES):
                     nc.tensor.matmul(
                         out=pw[:, mm, :],
-                        lhsT=w32[:, k, mm * P:(mm + 1) * P],
+                        lhsT=w32s[g][:, k, mm * P:(mm + 1) * P],
                         rhs=ident[:],
                         is_transpose=True,
                         start=(k == 0),
                         stop=(k == PLANES - 1),
                     )
-            return pw
+            sums[g] = pw
 
-        def w_cast(w32):
-            wg = gpool.tile([P, PASSES, WS, PACK], BF16, name="wg", align_bytes=64)
+        def w_cast(g):
+            width = units[g][2]
+            wg = gpool.tile([P, PASSES, width, PACK], BF16, name="wg", align_bytes=64)
             nc.vector.tensor_copy(
                 out=wg[:].rearrange("p h (c i) j -> p h c j i", i=4),
-                in_=w32[:].rearrange("p (h j) (c i) -> p h c j i", h=PASSES, i=4),
+                in_=w32s[g][:].rearrange("p (h j) (c i) -> p h c j i", h=PASSES, i=4),
             )
             return wg
 
-        def w_quant(wg):
-            wc = wq.tile([P, PASSES * WS], U32, name="wc", align_bytes=64)
-            wl = wq.tile([P, PASSES * WS], U8, name="wl", align_bytes=64)
+        def w_quant(g, wg):
+            width = units[g][2]
+            wc = wq.tile([P, PASSES * width], U32, name="wc", align_bytes=64)
+            wl = wq.tile([P, PASSES * width], U8, name="wl", align_bytes=64)
             nc.vector.quantize_mx(
                 out=wc[:].bitcast(FP8X4), scales=wl[:], in_=wg[:].rearrange("p h s j -> p (h s j)")
             )
-            return wc, wl
+            codes[g] = (wc, wl)
 
-        def w_bar(pw):
-            wsum = small.tile([P, MB], F32, name="wsum")
-            nc.vector.tensor_reduce(out=wsum[:], in_=pw[:], axis=AX.X, op=ALU.add)
-            wbar = small.tile([P, MB], F32, name="wbar")
+        def w_bar(g):
+            blocks = units[g][2] // P
+            wsum = small.tile([P, blocks], F32, name="wsum")
+            nc.vector.tensor_reduce(out=wsum[:], in_=sums[g][:], axis=AX.X, op=ALU.add)
+            wbar = small.tile([P, blocks], F32, name="wbar")
             nc.vector.tensor_scalar(out=wbar[:], in0=wsum[:], scalar1=2.0 ** -20, scalar2=None, op0=ALU.mult)
-            return wbar
+            bars[g] = wbar
 
-        def multiply(g, wc, wl, wbar):
-            b, u = divmod(g, UNITS)
-            for mm in range(MB):
-                o = outp.tile([P, N], F32, name="o")
+        def multiply(g):
+            b, s0, width = units[g]
+            wc, wl = codes[g]
+            for mm in range(width // P):
                 for nh in range(NH):
                     cols = slice(nh * NT, (nh + 1) * NT)
                     acc = ps_acc.tile([P, NT], F32, name="acc")
                     for h in range(PASSES):
-                        wcols = slice(h * WS + mm * P, h * WS + (mm + 1) * P)
+                        wcols = slice(h * width + mm * P, h * width + (mm + 1) * P)
                         nc.tensor.matmul_mx(
                             out=acc[:],
                             lhsT=wc[:, wcols].bitcast(FP8X4),
@@ -152,46 +169,74 @@ def tile_garnetlayer_t_kernel(tc, fi_v, d_av, out):
                             start=(h == 0),
                             stop=(h == PASSES - 1),
                         )
-                    if mm * NH + nh < MB * NH - ACT_EXITS[g]:
-                        nc.vector.tensor_scalar(
-                            out=o[:, cols], in0=acc[:], scalar1=wbar[:, mm:mm + 1], scalar2=None, op0=ALU.mult
-                        )
-                    else:
-                        nc.scalar.activation(out=o[:, cols], in_=acc[:], func=ACT.Copy, scale=wbar[:, mm:mm + 1])
-                nc.sync.dma_start(out=o_view[b, u * MB + mm], in_=o[:])
+                    accs[(g, mm * NH + nh)] = acc
 
-        load_d(0, [(0, WS), (WS, 2 * WS)])
-        load_f(0, 0)
-        for h in range(PASSES):
-            nc.sync.dma_start(out=d_raw[0][:, h, :, 2 * WS:S], in_=d_view[0, h][:, :, 2 * WS:S])
-        load_f(0, 1)
-        for b in range(1, GRAPHS):
-            load_f(b, 0)
-            load_f(b, 1)
-            load_d(b, [(0, S)])
+        def on_scalar(g, i):
+            return i >= (units[g][2] // P) * NH - ACT_EXITS[g]
 
-        total = GRAPHS * UNITS
-        w32s = {0: w_exp(0)}
-        f_tiles(0)
+        def exits(g, scalar_engine):
+            for i in range((units[g][2] // P) * NH):
+                if on_scalar(g, i) != scalar_engine:
+                    continue
+                mm, nh = divmod(i, NH)
+                if (g, mm) not in outs:
+                    outs[(g, mm)] = outp.tile([P, N], F32, name="o")
+                dst = outs[(g, mm)][:, nh * NT:(nh + 1) * NT]
+                if scalar_engine:
+                    nc.scalar.activation(out=dst, in_=accs[(g, i)][:], func=ACT.Copy, scale=bars[g][:, mm:mm + 1])
+                else:
+                    nc.vector.tensor_scalar(
+                        out=dst, in0=accs[(g, i)][:], scalar1=bars[g][:, mm:mm + 1], scalar2=None, op0=ALU.mult
+                    )
+
+        def stores(g):
+            b, s0, width = units[g]
+            for mm in range(width // P):
+                nc.sync.dma_start(out=o_view[b, s0 // P + mm], in_=outs[(g, mm)][:])
+
+        load_d(0, 0, 256)
+        load_f(0, 0, 0, NT)
+        load_f(0, 0, NT, N)
+        load_d(0, 256, 512)
+        load_f(0, 1, 0, NT)
+        load_f(0, 1, NT, N)
+        load_d(0, 512, S)
+        load_f(1, 0, 0, N)
+        load_d(1, 0, S)
+        load_f(1, 1, 0, N)
+        later = [("f", 2), ("d", 2), ("f", 3), ("d", 3)]
+
+        w_exp(0)
         fgs = {}
-        for piece in range(PASSES * NH):
+        for piece in range(PIECES):
             fgs[piece] = f_regroup(0, piece)
             if piece > 0:
                 f_quant(0, piece - 1, fgs[piece - 1])
-        f_quant(0, PASSES * NH - 1, fgs[PASSES * NH - 1])
-        for g in range(total):
-            b, u = divmod(g, UNITS)
+        f_quant(0, PIECES - 1, fgs[PIECES - 1])
+
+        for g in range(total + 1):
             if g + 1 < total:
-                w32s[g + 1] = w_exp(g + 1)
-            pw = w_sum_pe(w32s[g])
-            wg = w_cast(w32s[g])
-            fg = None
-            if b + 1 < GRAPHS:
-                if u == 0:
-                    f_tiles(b + 1)
-                fg = f_regroup(b + 1, u)
-            wc, wl = w_quant(wg)
-            if fg is not None:
-                f_quant(b + 1, u, fg)
-            wbar = w_bar(pw)
-            multiply(g, wc, wl, wbar)
+                w_exp(g + 1)
+            if g < total:
+                w_sum_pe(g)
+                wg = w_cast(g)
+                fg = None
+                if g < (GRAPHS - 1) * PIECES:
+                    fg = f_regroup(1 + g // PIECES, g % PIECES)
+                w_quant(g, wg)
+                if fg is not None:
+                    f_quant(1 + g // PIECES, g % PIECES, fg)
+                w_bar(g)
+                multiply(g)
+            if g >= 1:
+                exits(g - 1, False)
+                exits(g - 1, True)
+                stores(g - 1)
+                if later:
+                    kind, b = later[0]
+                    later = later[1:]
+                    if kind == "f":
+                        load_f(b, 0, 0, N)
+                        load_f(b, 1, 0, N)
+                    else:
+                        load_d(b, 0, S)

@@ -26,7 +26,8 @@ NT = 512
 NH = N // NT
 PIECES = PASSES * NH
 WIDTHS = [256] * 15 + [128, 128]
-ACT_EXITS = [3, 3, 2, 1, 1, 2, 1, 1, 1, 2, 1, 1, 1, 0, 3, 2, 0]
+ACT_EXITS = [2, 2, 2, 2, 1, 2, 1, 2, 1, 2, 1, 2, 1, 1, 1, 1, 1]
+LEAD = 2
 
 
 def tile_garnetlayer_t_kernel(tc, fi_v, d_av, out):
@@ -44,17 +45,16 @@ def tile_garnetlayer_t_kernel(tc, fi_v, d_av, out):
 
     with ExitStack() as ctx:
         const = ctx.enter_context(tc.tile_pool(name="const", bufs=1))
-        rawd = ctx.enter_context(tc.tile_pool(name="rawd", bufs=GRAPHS))
-        rawf = ctx.enter_context(tc.tile_pool(name="rawf", bufs=GRAPHS * PASSES))
-        wpool = ctx.enter_context(tc.tile_pool(name="wpool", bufs=3))
-        gpool = ctx.enter_context(tc.tile_pool(name="gpool", bufs=2))
-        wq = ctx.enter_context(tc.tile_pool(name="wq", bufs=3))
+        rawd = ctx.enter_context(tc.tile_pool(name="rawd", bufs=3))
+        rawf = ctx.enter_context(tc.tile_pool(name="rawf", bufs=6))
+        wpool = ctx.enter_context(tc.tile_pool(name="wpool", bufs=4))
+        gpool = ctx.enter_context(tc.tile_pool(name="gpool", bufs=3))
+        wq = ctx.enter_context(tc.tile_pool(name="wq", bufs=4))
         fq = ctx.enter_context(tc.tile_pool(name="fq", bufs=2))
         small = ctx.enter_context(tc.tile_pool(name="small", bufs=4))
-        outp = ctx.enter_context(tc.tile_pool(name="outp", bufs=6))
+        outp = ctx.enter_context(tc.tile_pool(name="outp", bufs=8))
         ps_sum = ctx.enter_context(tc.psum_pool(name="ps_sum", bufs=2))
         ps_acc = ctx.enter_context(tc.psum_pool(name="ps_acc", bufs=6))
-        ctx.enter_context(tc.manual_schedule())
 
         ident = const.tile([P, P], F32)
         make_identity(nc, ident[:])
@@ -148,8 +148,8 @@ def tile_garnetlayer_t_kernel(tc, fi_v, d_av, out):
             wsum = small.tile([P, blocks], F32, name="wsum")
             nc.vector.tensor_reduce(out=wsum[:], in_=sums[g][:], axis=AX.X, op=ALU.add)
             wbar = small.tile([P, blocks], F32, name="wbar")
-            nc.vector.tensor_scalar(out=wbar[:], in0=wsum[:], scalar1=2.0 ** -20, scalar2=None, op0=ALU.mult)
-            bars[g] = wbar
+            nc.gpsimd.tensor_scalar(out=wbar[:], in0=wsum[:], scalar1=2.0 ** -20, scalar2=0.0, op0=ALU.mult, op1=ALU.add)
+            bars[g] = (wsum, wbar)
 
         def multiply(g):
             b, s0, width = units[g]
@@ -183,10 +183,11 @@ def tile_garnetlayer_t_kernel(tc, fi_v, d_av, out):
                     outs[(g, mm)] = outp.tile([P, N], F32, name="o")
                 dst = outs[(g, mm)][:, nh * NT:(nh + 1) * NT]
                 if scalar_engine:
-                    nc.scalar.activation(out=dst, in_=accs[(g, i)][:], func=ACT.Copy, scale=bars[g][:, mm:mm + 1])
+                    nc.scalar.activation(out=dst, in_=accs[(g, i)][:], func=ACT.Copy, scale=bars[g][1][:, mm:mm + 1])
                 else:
                     nc.vector.tensor_scalar(
-                        out=dst, in0=accs[(g, i)][:], scalar1=bars[g][:, mm:mm + 1], scalar2=None, op0=ALU.mult
+                        out=dst, in0=accs[(g, i)][:], scalar1=bars[g][0][:, mm:mm + 1], scalar2=2.0 ** -20,
+                        op0=ALU.mult, op1=ALU.mult,
                     )
 
         def stores(g):
@@ -206,7 +207,8 @@ def tile_garnetlayer_t_kernel(tc, fi_v, d_av, out):
         load_f(1, 1, 0, N)
         later = [("f", 2), ("d", 2), ("f", 3), ("d", 3)]
 
-        w_exp(0)
+        for g in range(LEAD):
+            w_exp(g)
         fgs = {}
         for piece in range(PIECES):
             fgs[piece] = f_regroup(0, piece)
@@ -215,20 +217,17 @@ def tile_garnetlayer_t_kernel(tc, fi_v, d_av, out):
         f_quant(0, PIECES - 1, fgs[PIECES - 1])
 
         for g in range(total + 1):
-            if g + 1 < total:
-                w_exp(g + 1)
+            if g + LEAD < total:
+                w_exp(g + LEAD)
+            wg = None
+            fg = None
             if g < total:
                 w_sum_pe(g)
                 wg = w_cast(g)
-                fg = None
                 if g < (GRAPHS - 1) * PIECES:
                     fg = f_regroup(1 + g // PIECES, g % PIECES)
-                w_quant(g, wg)
-                if fg is not None:
-                    f_quant(1 + g // PIECES, g % PIECES, fg)
-                w_bar(g)
-                multiply(g)
             if g >= 1:
+                w_bar(g - 1)
                 exits(g - 1, False)
                 exits(g - 1, True)
                 stores(g - 1)
@@ -240,3 +239,8 @@ def tile_garnetlayer_t_kernel(tc, fi_v, d_av, out):
                         load_f(b, 1, 0, N)
                     else:
                         load_d(b, 0, S)
+            if g < total:
+                w_quant(g, wg)
+                if fg is not None:
+                    f_quant(1 + g // PIECES, g % PIECES, fg)
+                multiply(g)

@@ -25,8 +25,8 @@ PLANES = PASSES * PACK
 NT = 512
 NH = N // NT
 PIECES = PASSES * NH
-WIDTHS = [256] * 15 + [128, 128]
-ACT_EXITS = [2, 2, 2, 2, 1, 2, 1, 2, 1, 2, 1, 2, 1, 1, 1, 1, 1]
+WIDTHS = [128, 128] + [256] * 14 + [128, 128]
+ACT_EXITS = [1, 1, 2, 2, 2, 1, 2, 1, 2, 1, 2, 1, 2, 1, 1, 1, 1, 1]
 LEAD = 2
 
 
@@ -46,7 +46,8 @@ def tile_garnetlayer_t_kernel(tc, fi_v, d_av, out):
     with ExitStack() as ctx:
         const = ctx.enter_context(tc.tile_pool(name="const", bufs=1))
         rawd = ctx.enter_context(tc.tile_pool(name="rawd", bufs=3))
-        rawf = ctx.enter_context(tc.tile_pool(name="rawf", bufs=6))
+        rawf = ctx.enter_context(tc.tile_pool(name="rawf", bufs=4))
+        rawf0 = ctx.enter_context(tc.tile_pool(name="rawf0", bufs=PIECES))
         wpool = ctx.enter_context(tc.tile_pool(name="wpool", bufs=4))
         gpool = ctx.enter_context(tc.tile_pool(name="gpool", bufs=3))
         wq = ctx.enter_context(tc.tile_pool(name="wq", bufs=4))
@@ -56,11 +57,17 @@ def tile_garnetlayer_t_kernel(tc, fi_v, d_av, out):
         ps_sum = ctx.enter_context(tc.psum_pool(name="ps_sum", bufs=2))
         ps_acc = ctx.enter_context(tc.psum_pool(name="ps_acc", bufs=6))
 
+        zero = const.tile([P, 1], F32)
+        nc.vector.memset(zero[:], 0.0)
+        one = const.tile([P, 1], F32)
+        nc.scalar.activation(out=one[:], in_=zero[:], func=ACT.Exp)
+
         ident = const.tile([P, P], F32)
         make_identity(nc, ident[:])
 
         d_raw = {}
         f_raw = {}
+        f_first = {}
         f_codes = {}
         f_scales = {}
         w32s = {}
@@ -76,10 +83,14 @@ def tile_garnetlayer_t_kernel(tc, fi_v, d_av, out):
             for h in range(PASSES):
                 nc.sync.dma_start(out=d_raw[b][:, h, :, lo:hi], in_=d_view[b, h][:, :, lo:hi])
 
-        def load_f(b, h, lo, hi):
-            if (b, h) not in f_raw:
-                f_raw[(b, h)] = rawf.tile([P, PACK, N], BF16, name="f_raw")
-            nc.sync.dma_start(out=f_raw[(b, h)][:, :, lo:hi], in_=f_view[b, h][:, :, lo:hi])
+        def load_f(b, h):
+            f_raw[(b, h)] = rawf.tile([P, PACK, N], BF16, name="f_raw")
+            nc.sync.dma_start(out=f_raw[(b, h)][:], in_=f_view[b, h])
+
+        def load_f_piece(piece):
+            h, nh = divmod(piece, NH)
+            f_first[piece] = rawf0.tile([P, PACK, NT], BF16, name="f_first")
+            nc.sync.dma_start(out=f_first[piece][:], in_=f_view[0, h][:, :, nh * NT:(nh + 1) * NT])
 
         def f_regroup(b, piece):
             if b not in f_codes:
@@ -87,9 +98,10 @@ def tile_garnetlayer_t_kernel(tc, fi_v, d_av, out):
                 f_scales[b] = fq.tile([P, PASSES, N], U8, name="f_scales", align_bytes=64)
             h, nh = divmod(piece, NH)
             fg = gpool.tile([P, NT, PACK], BF16, name="fg", align_bytes=64)
+            rows = f_first[piece][:] if b == 0 else f_raw[(b, h)][:, :, nh * NT:(nh + 1) * NT]
             nc.vector.tensor_copy(
                 out=fg[:].rearrange("p (c i) t -> p c t i", i=4),
-                in_=f_raw[(b, h)][:, :, nh * NT:(nh + 1) * NT].rearrange("p t (c i) -> p c t i", i=4),
+                in_=rows.rearrange("p t (c i) -> p c t i", i=4),
             )
             return fg
 
@@ -193,18 +205,24 @@ def tile_garnetlayer_t_kernel(tc, fi_v, d_av, out):
         def stores(g):
             b, s0, width = units[g]
             for mm in range(width // P):
-                nc.sync.dma_start(out=o_view[b, s0 // P + mm], in_=outs[(g, mm)][:])
+                if g >= total - 2:
+                    for nh in range(NH):
+                        cols = slice(nh * NT, (nh + 1) * NT)
+                        nc.sync.dma_start(out=o_view[b, s0 // P + mm][:, cols], in_=outs[(g, mm)][:, cols])
+                else:
+                    nc.sync.dma_start(out=o_view[b, s0 // P + mm], in_=outs[(g, mm)][:])
 
-        load_d(0, 0, 256)
-        load_f(0, 0, 0, NT)
-        load_f(0, 0, NT, N)
+        load_d(0, 0, 128)
+        load_f_piece(0)
+        load_d(0, 128, 256)
+        load_f_piece(1)
         load_d(0, 256, 512)
-        load_f(0, 1, 0, NT)
-        load_f(0, 1, NT, N)
+        load_f_piece(2)
+        load_f_piece(3)
         load_d(0, 512, S)
-        load_f(1, 0, 0, N)
+        load_f(1, 0)
         load_d(1, 0, S)
-        load_f(1, 1, 0, N)
+        load_f(1, 1)
         later = [("f", 2), ("d", 2), ("f", 3), ("d", 3)]
 
         for g in range(LEAD):
@@ -224,8 +242,9 @@ def tile_garnetlayer_t_kernel(tc, fi_v, d_av, out):
             if g < total:
                 w_sum_pe(g)
                 wg = w_cast(g)
-                if g < (GRAPHS - 1) * PIECES:
-                    fg = f_regroup(1 + g // PIECES, g % PIECES)
+                turn = (units[g][0] * S + units[g][1]) // 256
+                if units[g][1] % 256 == 0 and turn < (GRAPHS - 1) * PIECES:
+                    fg = f_regroup(1 + turn // PIECES, turn % PIECES)
             if g >= 1:
                 w_bar(g - 1)
                 exits(g - 1, False)
@@ -235,12 +254,12 @@ def tile_garnetlayer_t_kernel(tc, fi_v, d_av, out):
                     kind, b = later[0]
                     later = later[1:]
                     if kind == "f":
-                        load_f(b, 0, 0, N)
-                        load_f(b, 1, 0, N)
+                        load_f(b, 0)
+                        load_f(b, 1)
                     else:
                         load_d(b, 0, S)
             if g < total:
                 w_quant(g, wg)
                 if fg is not None:
-                    f_quant(1 + g // PIECES, g % PIECES, fg)
+                    f_quant(1 + turn // PIECES, turn % PIECES, fg)
                 multiply(g)

@@ -12,7 +12,6 @@ U8 = mybir.dt.uint8
 FP8X4 = mybir.dt.float8_e4m3fn_x4
 ACT = mybir.ActivationFunctionType
 ALU = mybir.AluOpType
-AX = mybir.AxisListType
 
 P = 128
 PACK = 4
@@ -21,41 +20,41 @@ V = 1024
 S = 1024
 N = 1024
 PASSES = V // (P * PACK)
-PLANES = PASSES * PACK
+ROWS = V // P
 NT = 512
 NH = N // NT
 PIECES = PASSES * NH
-WIDTHS = [128, 128] + [256] * 14 + [128, 128]
-ACT_EXITS = [1, 1, 2, 2, 2, 1, 2, 1, 2, 1, 2, 1, 2, 1, 1, 1, 1, 1]
-LEAD = 2
+UNIT = 2 * P
+UPG = S // UNIT
+TOTAL = GRAPHS * UPG
+ACT_EXITS = {0: [3], 1: [3], 2: [3], 3: [3], 4: [3], 5: [3], 15: [1, 3]}
+LAST = TOTAL - 1
 
 
 def tile_garnetlayer_t_kernel(tc, fi_v, d_av, out):
     nc = tc.nc
-    d_view = d_av.rearrange("b (h p j) s -> b h p j s", h=PASSES, p=P, j=PACK)
+    d_view = d_av.rearrange("b (r p) s -> b p r s", p=P)
     f_view = fi_v.rearrange("b (h p j) n -> b h p j n", h=PASSES, p=P, j=PACK)
-    o_view = out.rearrange("b (m p n) -> b m p n", m=S // P, p=P, n=N)
-
-    units = []
-    start = 0
-    for width in WIDTHS:
-        units.append((start // S, start % S, width))
-        start += width
-    total = len(units)
+    o_view = out.rearrange("b (c q e n) -> b c q e n", c=UPG, q=P, e=2, n=N)
 
     with ExitStack() as ctx:
         const = ctx.enter_context(tc.tile_pool(name="const", bufs=1))
-        rawd = ctx.enter_context(tc.tile_pool(name="rawd", bufs=3))
+        rawd0 = ctx.enter_context(tc.tile_pool(name="rawd0", bufs=1))
+        rawd = ctx.enter_context(tc.tile_pool(name="rawd", bufs=4))
         rawf = ctx.enter_context(tc.tile_pool(name="rawf", bufs=4))
         rawf0 = ctx.enter_context(tc.tile_pool(name="rawf0", bufs=PIECES))
-        wpool = ctx.enter_context(tc.tile_pool(name="wpool", bufs=4))
-        gpool = ctx.enter_context(tc.tile_pool(name="gpool", bufs=3))
-        wq = ctx.enter_context(tc.tile_pool(name="wq", bufs=4))
+        sqp = ctx.enter_context(tc.tile_pool(name="sqp", bufs=2))
+        wtp = ctx.enter_context(tc.tile_pool(name="wtp", bufs=3))
+        wgp = ctx.enter_context(tc.tile_pool(name="wgp", bufs=2))
+        wq = ctx.enter_context(tc.tile_pool(name="wq", bufs=3))
+        fg0p = ctx.enter_context(tc.tile_pool(name="fg0p", bufs=2))
+        fgp = ctx.enter_context(tc.tile_pool(name="fgp", bufs=1))
         fq = ctx.enter_context(tc.tile_pool(name="fq", bufs=2))
-        small = ctx.enter_context(tc.tile_pool(name="small", bufs=4))
-        outp = ctx.enter_context(tc.tile_pool(name="outp", bufs=8))
-        ps_sum = ctx.enter_context(tc.psum_pool(name="ps_sum", bufs=2))
-        ps_acc = ctx.enter_context(tc.psum_pool(name="ps_acc", bufs=6))
+        small = ctx.enter_context(tc.tile_pool(name="small", bufs=6))
+        outp = ctx.enter_context(tc.tile_pool(name="outp", bufs=5))
+        ps_d = ctx.enter_context(tc.psum_pool(name="ps_d", bufs=2))
+        ps_w = ctx.enter_context(tc.psum_pool(name="ps_w", bufs=2))
+        ps_acc = ctx.enter_context(tc.psum_pool(name="ps_acc", bufs=4))
 
         zero = const.tile([P, 1], F32)
         nc.vector.memset(zero[:], 0.0)
@@ -70,196 +69,243 @@ def tile_garnetlayer_t_kernel(tc, fi_v, d_av, out):
         f_first = {}
         f_codes = {}
         f_scales = {}
-        w32s = {}
-        sums = {}
-        codes = {}
+        fgs = {}
+        wts = {}
         bars = {}
+        wps = {}
+        wgs = {}
+        codes = {}
         accs = {}
         outs = {}
 
-        def load_d(b, lo, hi):
-            if b not in d_raw:
-                d_raw[b] = rawd.tile([P, PASSES, PACK, S], BF16, name="d_raw")
-            for h in range(PASSES):
-                nc.sync.dma_start(out=d_raw[b][:, h, :, lo:hi], in_=d_view[b, h][:, :, lo:hi])
+        def load_d_first(c, h):
+            piece = rawd0.tile([P, PACK, UNIT], BF16, name="d_first_%d_%d" % (c, h))
+            nc.sync.dma_start(
+                out=piece[:], in_=d_view[0][:, PACK * h:PACK * (h + 1), c * UNIT:(c + 1) * UNIT]
+            )
+            for r in range(PACK):
+                d_raw[(c, PACK * h + r)] = piece[:, r, :]
+
+        def load_d(b, half):
+            piece = rawd.tile([P, ROWS, S // 2], BF16, name="d_half")
+            nc.sync.dma_start(out=piece[:], in_=d_view[b][:, :, half * (S // 2):(half + 1) * (S // 2)])
+            for c in range(2):
+                for r in range(ROWS):
+                    d_raw[(b * UPG + 2 * half + c, r)] = piece[:, r, c * UNIT:(c + 1) * UNIT]
 
         def load_f(b, h):
             f_raw[(b, h)] = rawf.tile([P, PACK, N], BF16, name="f_raw")
             nc.sync.dma_start(out=f_raw[(b, h)][:], in_=f_view[b, h])
 
-        def load_f_piece(piece):
-            h, nh = divmod(piece, NH)
-            f_first[piece] = rawf0.tile([P, PACK, NT], BF16, name="f_first")
-            nc.sync.dma_start(out=f_first[piece][:], in_=f_view[0, h][:, :, nh * NT:(nh + 1) * NT])
+        def load_f_piece(h, nh):
+            f_first[(h, nh)] = rawf0.tile([P, PACK, NT], BF16, name="f_first")
+            nc.sync.dma_start(out=f_first[(h, nh)][:], in_=f_view[0, h][:, :, nh * NT:(nh + 1) * NT])
 
-        def f_regroup(b, piece):
+        def f_regroup_first(h, nh):
+            fg = fg0p.tile([P, NT, PACK], BF16, name="fg0", align_bytes=64)
+            nc.vector.tensor_copy(
+                out=fg[:].rearrange("p (c i) t -> p c t i", i=4),
+                in_=f_first[(h, nh)][:].rearrange("p t (c i) -> p c t i", i=4),
+            )
+            fgs[(0, h, nh)] = fg
+
+        def f_regroup_pool(b, h, nh):
+            fg = fgp.tile([P, NT, PACK], BF16, name="fg", align_bytes=64)
+            nc.gpsimd.tensor_scalar(
+                out=fg[:],
+                in0=f_raw[(b, h)][:, :, nh * NT:(nh + 1) * NT].rearrange("p t n -> p n t"),
+                scalar1=1.0, scalar2=0.0, op0=ALU.mult, op1=ALU.add,
+            )
+            fgs[(b, h, nh)] = fg
+
+        def f_quant(b, h, nh):
             if b not in f_codes:
                 f_codes[b] = fq.tile([P, PASSES, N], U32, name="f_codes", align_bytes=64)
                 f_scales[b] = fq.tile([P, PASSES, N], U8, name="f_scales", align_bytes=64)
-            h, nh = divmod(piece, NH)
-            fg = gpool.tile([P, NT, PACK], BF16, name="fg", align_bytes=64)
-            rows = f_first[piece][:] if b == 0 else f_raw[(b, h)][:, :, nh * NT:(nh + 1) * NT]
-            nc.vector.tensor_copy(
-                out=fg[:].rearrange("p (c i) t -> p c t i", i=4),
-                in_=rows.rearrange("p t (c i) -> p c t i", i=4),
-            )
-            return fg
-
-        def f_quant(b, piece, fg):
-            h, nh = divmod(piece, NH)
             cols = slice(nh * NT, (nh + 1) * NT)
             nc.vector.quantize_mx(
                 out=f_codes[b][:, h, cols].bitcast(FP8X4),
                 scales=f_scales[b][:, h, cols],
-                in_=fg[:].rearrange("p n t -> p (n t)"),
+                in_=fgs[(b, h, nh)][:].rearrange("p n t -> p (n t)"),
             )
 
-        def w_exp(g):
-            b, s0, width = units[g]
-            w32 = wpool.tile([P, PLANES, width], F32, name="w32")
-            src = d_raw[b][:].rearrange("p h j s -> p (h j) s")[:, :, s0:s0 + width]
-            nc.scalar.activation(out=w32[:], in_=src, func=ACT.Square)
-            nc.scalar.activation(out=w32[:], in_=w32[:], func=ACT.Exp, scale=-1.0)
-            w32s[g] = w32
-
-        def w_sum_pe(g):
-            blocks = units[g][2] // P
-            pw = ps_sum.tile([P, blocks, P], F32, name="pw")
-            for mm in range(blocks):
-                for k in range(PLANES):
-                    nc.tensor.matmul(
-                        out=pw[:, mm, :],
-                        lhsT=w32s[g][:, k, mm * P:(mm + 1) * P],
-                        rhs=ident[:],
-                        is_transpose=True,
-                        start=(k == 0),
-                        stop=(k == PLANES - 1),
+        def stage_a(g):
+            b, c = divmod(g, UPG)
+            sq = sqp.tile([P, 2, V], F32, name="sq")
+            for h in range(PASSES):
+                dt = ps_d.tile([P, PACK, P], F32, name="dt")
+                for r in range(PACK):
+                    nc.tensor.transpose(
+                        dt[:, r, :], d_raw[(g, PACK * h + r)].bitcast(F32), ident[:]
                     )
-            sums[g] = pw
+                turned = dt[:].rearrange("q r p -> q (r p)").bitcast(BF16).rearrange(
+                    "q (x u f e) -> q e u x f", x=P, u=2, f=2, e=2)
+                for e in range(2):
+                    nc.scalar.activation(
+                        out=sq[:, e, h * 512:(h + 1) * 512].rearrange("q (u x f) -> q u x f", u=2, x=P, f=2),
+                        in_=turned[:, e],
+                        func=ACT.Square,
+                    )
+            wt = wtp.tile([P, 2, V], BF16, name="wt")
+            wsum = small.tile([P, 2], F32, name="wsum")
+            for e in range(2):
+                nc.scalar.activation(
+                    out=wt[:, e, :], in_=sq[:, e, :], func=ACT.Exp, scale=-1.0, accum_out=wsum[:, e:e + 1]
+                )
+            wts[g] = wt
+            bars[g] = [wsum, None]
 
-        def w_cast(g):
-            width = units[g][2]
-            wg = gpool.tile([P, PASSES, width, PACK], BF16, name="wg", align_bytes=64)
-            nc.vector.tensor_copy(
-                out=wg[:].rearrange("p h (c i) j -> p h c j i", i=4),
-                in_=w32s[g][:].rearrange("p (h j) (c i) -> p h c j i", h=PASSES, i=4),
+        def w_scale(g):
+            wbar = small.tile([P, 2], F32, name="wbar")
+            nc.gpsimd.tensor_scalar(
+                out=wbar[:], in0=bars[g][0][:], scalar1=2.0 ** -20, scalar2=0.0, op0=ALU.mult, op1=ALU.add
             )
-            return wg
+            bars[g][1] = wbar
 
-        def w_quant(g, wg):
-            width = units[g][2]
-            wc = wq.tile([P, PASSES * width], U32, name="wc", align_bytes=64)
-            wl = wq.tile([P, PASSES * width], U8, name="wl", align_bytes=64)
+        def w_turn(g, e):
+            wp = ps_w.tile([P, PACK, P], F32, name="wp")
+            for k in range(PACK):
+                nc.tensor.transpose(wp[:, k, :], wts[g][:, e, k * 256:(k + 1) * 256].bitcast(F32), ident[:])
+            wps[(g, e)] = wp
+
+        def w_copy(g, e):
+            if g not in wgs:
+                wgs[g] = wgp.tile([P, 2, PASSES, P, 2], F32, name="wg", align_bytes=64)
+            nc.vector.tensor_copy(
+                out=wgs[g][:, e], in_=wps[(g, e)][:].rearrange("p (h u) q -> p h q u", h=PASSES)
+            )
+
+        def w_quant(g):
+            wc = wq.tile([P, 2 * PASSES * P], U32, name="wc", align_bytes=64)
+            wl = wq.tile([P, 2 * PASSES * P], U8, name="wl", align_bytes=64)
             nc.vector.quantize_mx(
-                out=wc[:].bitcast(FP8X4), scales=wl[:], in_=wg[:].rearrange("p h s j -> p (h s j)")
+                out=wc[:].bitcast(FP8X4), scales=wl[:],
+                in_=wgs[g][:].rearrange("p e h q u -> p (e h q u)").bitcast(BF16),
             )
             codes[g] = (wc, wl)
 
-        def w_bar(g):
-            blocks = units[g][2] // P
-            wsum = small.tile([P, blocks], F32, name="wsum")
-            nc.vector.tensor_reduce(out=wsum[:], in_=sums[g][:], axis=AX.X, op=ALU.add)
-            wbar = small.tile([P, blocks], F32, name="wbar")
-            nc.gpsimd.tensor_scalar(out=wbar[:], in0=wsum[:], scalar1=2.0 ** -20, scalar2=0.0, op0=ALU.mult, op1=ALU.add)
-            bars[g] = (wsum, wbar)
-
-        def multiply(g):
-            b, s0, width = units[g]
+        def w_quant_half(g, e):
+            if g not in codes:
+                wc = wq.tile([P, 2 * PASSES * P], U32, name="wc", align_bytes=64)
+                wl = wq.tile([P, 2 * PASSES * P], U8, name="wl", align_bytes=64)
+                codes[g] = (wc, wl)
             wc, wl = codes[g]
-            for mm in range(width // P):
-                for nh in range(NH):
-                    cols = slice(nh * NT, (nh + 1) * NT)
-                    acc = ps_acc.tile([P, NT], F32, name="acc")
-                    for h in range(PASSES):
-                        wcols = slice(h * width + mm * P, h * width + (mm + 1) * P)
-                        nc.tensor.matmul_mx(
-                            out=acc[:],
-                            lhsT=wc[:, wcols].bitcast(FP8X4),
-                            lhsT_scale=wl[:, wcols],
-                            rhs=f_codes[b][:, h, cols].bitcast(FP8X4),
-                            rhs_scale=f_scales[b][:, h, cols],
-                            start=(h == 0),
-                            stop=(h == PASSES - 1),
-                        )
-                    accs[(g, mm * NH + nh)] = acc
+            cols = slice(e * PASSES * P, (e + 1) * PASSES * P)
+            nc.vector.quantize_mx(
+                out=wc[:, cols].bitcast(FP8X4), scales=wl[:, cols],
+                in_=wgs[g][:, e].rearrange("p h q u -> p (h q u)").bitcast(BF16),
+            )
 
-        def on_scalar(g, i):
-            return i >= (units[g][2] // P) * NH - ACT_EXITS[g]
+        def multiply(g, e):
+            b = g // UPG
+            wc, wl = codes[g]
+            for nh in range(NH):
+                cols = slice(nh * NT, (nh + 1) * NT)
+                acc = ps_acc.tile([P, NT], F32, name="acc")
+                for h in range(PASSES):
+                    wcols = slice((e * PASSES + h) * P, (e * PASSES + h + 1) * P)
+                    nc.tensor.matmul_mx(
+                        out=acc[:],
+                        lhsT=wc[:, wcols].bitcast(FP8X4),
+                        lhsT_scale=wl[:, wcols],
+                        rhs=f_codes[b][:, h, cols].bitcast(FP8X4),
+                        rhs_scale=f_scales[b][:, h, cols],
+                        start=(h == 0),
+                        stop=(h == PASSES - 1),
+                    )
+                accs[(g, e * NH + nh)] = acc
 
-        def exits(g, scalar_engine):
-            for i in range((units[g][2] // P) * NH):
-                if on_scalar(g, i) != scalar_engine:
-                    continue
-                mm, nh = divmod(i, NH)
-                if (g, mm) not in outs:
-                    outs[(g, mm)] = outp.tile([P, N], F32, name="o")
-                dst = outs[(g, mm)][:, nh * NT:(nh + 1) * NT]
-                if scalar_engine:
-                    nc.scalar.activation(out=dst, in_=accs[(g, i)][:], func=ACT.Copy, scale=bars[g][1][:, mm:mm + 1])
+        def exits(g, e):
+            b, c = divmod(g, UPG)
+            if g not in outs:
+                outs[g] = outp.tile([P, 2, N], F32, name="o")
+            for nh in range(NH):
+                i = e * NH + nh
+                dst = outs[g][:, e, nh * NT:(nh + 1) * NT]
+                if i in ACT_EXITS.get(g, []):
+                    nc.scalar.activation(out=dst, in_=accs[(g, i)][:], func=ACT.Copy, scale=bars[g][1][:, e:e + 1])
                 else:
                     nc.vector.tensor_scalar(
-                        out=dst, in0=accs[(g, i)][:], scalar1=bars[g][0][:, mm:mm + 1], scalar2=2.0 ** -20,
+                        out=dst, in0=accs[(g, i)][:], scalar1=bars[g][0][:, e:e + 1], scalar2=2.0 ** -20,
                         op0=ALU.mult, op1=ALU.mult,
                     )
+                if g == LAST:
+                    cols = slice(nh * NT, (nh + 1) * NT)
+                    nc.sync.dma_start(out=o_view[b, c][:, e, cols], in_=outs[g][:, e, cols])
+            if g != LAST:
+                nc.sync.dma_start(out=o_view[b, c][:, e, :], in_=outs[g][:, e, :])
 
-        def stores(g):
-            b, s0, width = units[g]
-            for mm in range(width // P):
-                if g >= total - 2:
-                    for nh in range(NH):
-                        cols = slice(nh * NT, (nh + 1) * NT)
-                        nc.sync.dma_start(out=o_view[b, s0 // P + mm][:, cols], in_=outs[(g, mm)][:, cols])
-                else:
-                    nc.sync.dma_start(out=o_view[b, s0 // P + mm], in_=outs[(g, mm)][:])
-
-        load_d(0, 0, 128)
-        load_f_piece(0)
-        load_d(0, 128, 256)
-        load_f_piece(1)
-        load_d(0, 256, 512)
-        load_f_piece(2)
-        load_f_piece(3)
-        load_d(0, 512, S)
+        load_d_first(0, 0)
+        load_d_first(0, 1)
+        load_f_piece(0, 0)
+        load_d_first(1, 0)
+        load_d_first(1, 1)
+        load_f_piece(1, 0)
+        load_f_piece(0, 1)
+        load_f_piece(1, 1)
+        load_d_first(2, 0)
+        load_d_first(2, 1)
+        load_d_first(3, 0)
+        load_d_first(3, 1)
         load_f(1, 0)
-        load_d(1, 0, S)
         load_f(1, 1)
-        later = [("f", 2), ("d", 2), ("f", 3), ("d", 3)]
+        load_d(1, 0)
+        later = [("f", 2, 0), ("d", 1, 1), ("f", 2, 1), ("d", 2, 0), ("f", 3, 0), ("d", 2, 1), ("f", 3, 1),
+                 ("d", 3, 0), ("d", 3, 1)]
 
-        for g in range(LEAD):
-            w_exp(g)
-        fgs = {}
-        for piece in range(PIECES):
-            fgs[piece] = f_regroup(0, piece)
-            if piece > 0:
-                f_quant(0, piece - 1, fgs[piece - 1])
-        f_quant(0, PIECES - 1, fgs[PIECES - 1])
+        stage_a(0)
+        f_regroup_first(0, 0)
+        f_regroup_first(1, 0)
+        f_quant(0, 0, 0)
+        f_quant(0, 1, 0)
 
-        for g in range(total + 1):
-            if g + LEAD < total:
-                w_exp(g + LEAD)
-            wg = None
-            fg = None
-            if g < total:
-                w_sum_pe(g)
-                wg = w_cast(g)
-                turn = (units[g][0] * S + units[g][1]) // 256
-                if units[g][1] % 256 == 0 and turn < (GRAPHS - 1) * PIECES:
-                    fg = f_regroup(1 + turn // PIECES, turn % PIECES)
-            if g >= 1:
-                w_bar(g - 1)
-                exits(g - 1, False)
-                exits(g - 1, True)
-                stores(g - 1)
-                if later:
-                    kind, b = later[0]
-                    later = later[1:]
-                    if kind == "f":
-                        load_f(b, 0)
-                        load_f(b, 1)
-                    else:
-                        load_d(b, 0, S)
-            if g < total:
-                w_quant(g, wg)
-                if fg is not None:
-                    f_quant(1 + turn // PIECES, turn % PIECES, fg)
-                multiply(g)
+        def piece(j):
+            return 1 + j // PIECES, (j % PIECES) // NH, j % NH
+
+        for i in range(-1, TOTAL):
+            nxt = i + 1
+            if i + 2 < TOTAL:
+                stage_a(i + 2)
+            if nxt == LAST:
+                w_scale(nxt)
+                for e in range(2):
+                    w_turn(nxt, e)
+                    w_copy(nxt, e)
+                    exits(i, e)
+                    w_quant_half(nxt, e)
+                    multiply(nxt, e)
+                continue
+            if nxt < TOTAL:
+                if ACT_EXITS.get(nxt):
+                    w_scale(nxt)
+                w_turn(nxt, 0)
+                w_turn(nxt, 1)
+                w_copy(nxt, 0)
+                w_copy(nxt, 1)
+            if i >= 0:
+                exits(i, 0)
+            if i == -1:
+                f_regroup_first(0, 1)
+            if nxt < TOTAL:
+                w_quant(nxt)
+            if i == -1:
+                f_regroup_first(1, 1)
+                f_quant(0, 0, 1)
+                f_quant(0, 1, 1)
+            if 0 <= i < (GRAPHS - 1) * PIECES:
+                f_quant(*piece(i))
+            if nxt < (GRAPHS - 1) * PIECES:
+                f_regroup_pool(*piece(nxt))
+            if nxt < TOTAL:
+                multiply(nxt, 0)
+            if i >= 0:
+                exits(i, 1)
+            if nxt < TOTAL:
+                multiply(nxt, 1)
+            if later:
+                kind, b, half = later[0]
+                later = later[1:]
+                if kind == "f":
+                    load_f(b, half)
+                else:
+                    load_d(b, half)

@@ -27,7 +27,7 @@ PIECES = PASSES * NH
 UNIT = 2 * P
 UPG = S // UNIT
 TOTAL = GRAPHS * UPG
-ACT_EXITS = {0: [3], 1: [3], 2: [3], 3: [3], 4: [3], 5: [3], 15: [1, 3]}
+ACT_EXITS = {14: [3], 15: [1, 3]}
 LAST = TOTAL - 1
 
 
@@ -55,6 +55,7 @@ def tile_garnetlayer_t_kernel(tc, fi_v, d_av, out):
         ps_d = ctx.enter_context(tc.psum_pool(name="ps_d", bufs=2))
         ps_w = ctx.enter_context(tc.psum_pool(name="ps_w", bufs=2))
         ps_acc = ctx.enter_context(tc.psum_pool(name="ps_acc", bufs=4))
+        ctx.enter_context(tc.manual_schedule())
 
         zero = const.tile([P, 1], F32)
         nc.vector.memset(zero[:], 0.0)
@@ -70,6 +71,7 @@ def tile_garnetlayer_t_kernel(tc, fi_v, d_av, out):
         f_codes = {}
         f_scales = {}
         fgs = {}
+        dts = {}
         wts = {}
         bars = {}
         wps = {}
@@ -129,16 +131,19 @@ def tile_garnetlayer_t_kernel(tc, fi_v, d_av, out):
                 in_=fgs[(b, h, nh)][:].rearrange("p n t -> p (n t)"),
             )
 
-        def stage_a(g):
-            b, c = divmod(g, UPG)
-            sq = sqp.tile([P, 2, V], F32, name="sq")
+        def d_turn(g):
             for h in range(PASSES):
                 dt = ps_d.tile([P, PACK, P], F32, name="dt")
                 for r in range(PACK):
                     nc.tensor.transpose(
                         dt[:, r, :], d_raw[(g, PACK * h + r)].bitcast(F32), ident[:]
                     )
-                turned = dt[:].rearrange("q r p -> q (r p)").bitcast(BF16).rearrange(
+                dts[(g, h)] = dt
+
+        def stage_a(g):
+            sq = sqp.tile([P, 2, V], F32, name="sq")
+            for h in range(PASSES):
+                turned = dts[(g, h)][:].rearrange("q r p -> q (r p)").bitcast(BF16).rearrange(
                     "q (x u f e) -> q e u x f", x=P, u=2, f=2, e=2)
                 for e in range(2):
                     nc.scalar.activation(
@@ -232,7 +237,10 @@ def tile_garnetlayer_t_kernel(tc, fi_v, d_av, out):
                 if g == LAST:
                     cols = slice(nh * NT, (nh + 1) * NT)
                     nc.sync.dma_start(out=o_view[b, c][:, e, cols], in_=outs[g][:, e, cols])
-            if g != LAST:
+
+        def store(g):
+            b, c = divmod(g, UPG)
+            for e in range(2):
                 nc.sync.dma_start(out=o_view[b, c][:, e, :], in_=outs[g][:, e, :])
 
         load_d_first(0, 0)
@@ -245,67 +253,77 @@ def tile_garnetlayer_t_kernel(tc, fi_v, d_av, out):
         load_f_piece(1, 1)
         load_d_first(2, 0)
         load_d_first(2, 1)
+        load_f(1, 0)
         load_d_first(3, 0)
         load_d_first(3, 1)
-        load_f(1, 0)
-        load_f(1, 1)
         load_d(1, 0)
-        later = [("f", 2, 0), ("d", 1, 1), ("f", 2, 1), ("d", 2, 0), ("f", 3, 0), ("d", 2, 1), ("f", 3, 1),
-                 ("d", 3, 0), ("d", 3, 1)]
-
-        stage_a(0)
-        f_regroup_first(0, 0)
-        f_regroup_first(1, 0)
-        f_quant(0, 0, 0)
-        f_quant(0, 1, 0)
+        load_f(1, 1)
+        later = [("d", 1, 1), ("f", 2, 0), ("d", 2, 0), ("f", 2, 1), ("d", 2, 1), ("f", 3, 0), ("d", 3, 0),
+                 ("f", 3, 1), ("d", 3, 1)]
 
         def piece(j):
             return 1 + j // PIECES, (j % PIECES) // NH, j % NH
 
-        for i in range(-1, TOTAL):
-            nxt = i + 1
-            if i + 2 < TOTAL:
-                stage_a(i + 2)
-            if nxt == LAST:
-                w_scale(nxt)
-                for e in range(2):
-                    w_turn(nxt, e)
-                    w_copy(nxt, e)
-                    exits(i, e)
-                    w_quant_half(nxt, e)
-                    multiply(nxt, e)
-                continue
-            if nxt < TOTAL:
-                if ACT_EXITS.get(nxt):
-                    w_scale(nxt)
-                w_turn(nxt, 0)
-                w_turn(nxt, 1)
-                w_copy(nxt, 0)
-                w_copy(nxt, 1)
-            if i >= 0:
-                exits(i, 0)
-            if i == -1:
+        pieces = (GRAPHS - 1) * PIECES
+        d_turn(0)
+        for c in range(TOTAL):
+            turned_unit = c - 1
+            done_unit = c - 2
+            stage_a(c)
+            if c == 0:
+                f_regroup_first(0, 0)
+                f_regroup_first(1, 0)
+                f_quant(0, 0, 0)
                 f_regroup_first(0, 1)
-            if nxt < TOTAL:
-                w_quant(nxt)
-            if i == -1:
+                f_quant(0, 1, 0)
                 f_regroup_first(1, 1)
                 f_quant(0, 0, 1)
+            if turned_unit >= 0:
+                w_turn(turned_unit, 0)
+                w_turn(turned_unit, 1)
+                w_copy(turned_unit, 0)
+                w_copy(turned_unit, 1)
+            if c == 1:
                 f_quant(0, 1, 1)
-            if 0 <= i < (GRAPHS - 1) * PIECES:
-                f_quant(*piece(i))
-            if nxt < (GRAPHS - 1) * PIECES:
-                f_regroup_pool(*piece(nxt))
-            if nxt < TOTAL:
-                multiply(nxt, 0)
-            if i >= 0:
-                exits(i, 1)
-            if nxt < TOTAL:
-                multiply(nxt, 1)
-            if later:
+            if done_unit >= 0:
+                multiply(done_unit, 0)
+                multiply(done_unit, 1)
+                exits(done_unit, 0)
+            if turned_unit >= 0:
+                w_quant(turned_unit)
+            if 0 <= c - 2 < pieces:
+                f_quant(*piece(c - 2))
+            if 0 <= c - 1 < pieces:
+                f_regroup_pool(*piece(c - 1))
+            if done_unit >= 0:
+                exits(done_unit, 1)
+            if c + 1 < TOTAL:
+                d_turn(c + 1)
+            if c >= 3:
+                store(c - 3)
+            if c >= 1 and later:
                 kind, b, half = later[0]
                 later = later[1:]
                 if kind == "f":
                     load_f(b, half)
                 else:
                     load_d(b, half)
+
+        w_scale(LAST - 1)
+        w_scale(LAST)
+        store(LAST - 2)
+        multiply(LAST - 1, 0)
+        multiply(LAST - 1, 1)
+        w_turn(LAST, 0)
+        w_copy(LAST, 0)
+        exits(LAST - 1, 0)
+        w_quant_half(LAST, 0)
+        w_turn(LAST, 1)
+        w_copy(LAST, 1)
+        multiply(LAST, 0)
+        exits(LAST - 1, 1)
+        w_quant_half(LAST, 1)
+        multiply(LAST, 1)
+        store(LAST - 1)
+        exits(LAST, 0)
+        exits(LAST, 1)

@@ -27,7 +27,7 @@ PIECES = PASSES * NH
 UNIT = 2 * P
 UPG = S // UNIT
 TOTAL = GRAPHS * UPG
-ACT_EXITS = {14: [3], 15: [1, 3]}
+ACT_EXITS = {14: [1, 3], 15: [1, 3]}
 LAST = TOTAL - 1
 
 
@@ -221,11 +221,15 @@ def tile_garnetlayer_t_kernel(tc, fi_v, d_av, out):
                 accs[(g, e * NH + nh)] = acc
 
         def exits(g, e):
+            for nh in range(NH):
+                leave(g, e * NH + nh)
+
+        def leave(g, i):
             b, c = divmod(g, UPG)
+            e, nh = divmod(i, NH)
             if g not in outs:
                 outs[g] = outp.tile([P, 2, N], F32, name="o")
-            for nh in range(NH):
-                i = e * NH + nh
+            if True:
                 dst = outs[g][:, e, nh * NT:(nh + 1) * NT]
                 if i in ACT_EXITS.get(g, []):
                     nc.scalar.activation(out=dst, in_=accs[(g, i)][:], func=ACT.Copy, scale=bars[g][1][:, e:e + 1])
@@ -279,6 +283,8 @@ def tile_garnetlayer_t_kernel(tc, fi_v, d_av, out):
                 f_regroup_first(1, 1)
                 f_quant(0, 0, 1)
             if turned_unit >= 0:
+                if ACT_EXITS.get(turned_unit):
+                    w_scale(turned_unit)
                 w_turn(turned_unit, 0)
                 w_turn(turned_unit, 1)
                 w_copy(turned_unit, 0)
@@ -288,8 +294,12 @@ def tile_garnetlayer_t_kernel(tc, fi_v, d_av, out):
             if done_unit >= 0:
                 multiply(done_unit, 0)
                 multiply(done_unit, 1)
-                exits(done_unit, 0)
-            if turned_unit >= 0:
+                leave(done_unit, 0)
+            if c - 2 >= pieces:
+                w_quant(turned_unit)
+            if done_unit >= 0:
+                leave(done_unit, 1)
+            if turned_unit >= 0 and c - 2 < pieces:
                 w_quant(turned_unit)
             if 0 <= c - 2 < pieces:
                 f_quant(*piece(c - 2))
@@ -309,16 +319,15 @@ def tile_garnetlayer_t_kernel(tc, fi_v, d_av, out):
                 else:
                     load_d(b, half)
 
-        w_scale(LAST - 1)
         w_scale(LAST)
         store(LAST - 2)
-        multiply(LAST - 1, 0)
-        multiply(LAST - 1, 1)
         w_turn(LAST, 0)
+        multiply(LAST - 1, 0)
+        w_turn(LAST, 1)
+        multiply(LAST - 1, 1)
         w_copy(LAST, 0)
         exits(LAST - 1, 0)
         w_quant_half(LAST, 0)
-        w_turn(LAST, 1)
         w_copy(LAST, 1)
         multiply(LAST, 0)
         exits(LAST - 1, 1)

@@ -27,7 +27,7 @@ PIECES = PASSES * NH
 UNIT = 2 * P
 UPG = S // UNIT
 TOTAL = GRAPHS * UPG
-ACT_EXITS = {14: [1, 3], 15: [1, 3]}
+ACT_EXITS = {14: [0, 1, 2, 3], 15: [1, 3]}
 LAST = TOTAL - 1
 
 
@@ -131,8 +131,8 @@ def tile_garnetlayer_t_kernel(tc, fi_v, d_av, out):
                 in_=fgs[(b, h, nh)][:].rearrange("p n t -> p (n t)"),
             )
 
-        def d_turn(g):
-            for h in range(PASSES):
+        def d_turn(g, halves):
+            for h in halves:
                 dt = ps_d.tile([P, PACK, P], F32, name="dt")
                 for r in range(PACK):
                     nc.tensor.transpose(
@@ -269,7 +269,7 @@ def tile_garnetlayer_t_kernel(tc, fi_v, d_av, out):
             return 1 + j // PIECES, (j % PIECES) // NH, j % NH
 
         pieces = (GRAPHS - 1) * PIECES
-        d_turn(0)
+        d_turn(0, [0, 1])
         for c in range(TOTAL):
             turned_unit = c - 1
             done_unit = c - 2
@@ -293,6 +293,9 @@ def tile_garnetlayer_t_kernel(tc, fi_v, d_av, out):
                 f_quant(0, 1, 1)
             if done_unit >= 0:
                 multiply(done_unit, 0)
+            if c + 1 < TOTAL:
+                d_turn(c + 1, [0])
+            if done_unit >= 0:
                 multiply(done_unit, 1)
                 leave(done_unit, 0)
             if c - 2 >= pieces:
@@ -308,7 +311,7 @@ def tile_garnetlayer_t_kernel(tc, fi_v, d_av, out):
             if done_unit >= 0:
                 exits(done_unit, 1)
             if c + 1 < TOTAL:
-                d_turn(c + 1)
+                d_turn(c + 1, [1])
             if c >= 3:
                 store(c - 3)
             if c >= 1 and later:
@@ -327,8 +330,8 @@ def tile_garnetlayer_t_kernel(tc, fi_v, d_av, out):
         multiply(LAST - 1, 1)
         w_copy(LAST, 0)
         exits(LAST - 1, 0)
-        w_quant_half(LAST, 0)
         w_copy(LAST, 1)
+        w_quant_half(LAST, 0)
         multiply(LAST, 0)
         exits(LAST - 1, 1)
         w_quant_half(LAST, 1)

@@ -250,9 +250,9 @@ def tile_garnetlayer_t_kernel(tc, fi_v, d_av, out):
         load_d_first(0, 0)
         load_d_first(0, 1)
         load_f_piece(0, 0)
+        load_f_piece(1, 0)
         load_d_first(1, 0)
         load_d_first(1, 1)
-        load_f_piece(1, 0)
         load_f_piece(0, 1)
         load_f_piece(1, 1)
         load_d_first(2, 0)
@@ -278,19 +278,19 @@ def tile_garnetlayer_t_kernel(tc, fi_v, d_av, out):
                 f_regroup_first(0, 0)
                 f_regroup_first(1, 0)
                 f_quant(0, 0, 0)
-                f_regroup_first(0, 1)
                 f_quant(0, 1, 0)
-                f_regroup_first(1, 1)
-                f_quant(0, 0, 1)
             if turned_unit >= 0:
                 if ACT_EXITS.get(turned_unit):
                     w_scale(turned_unit)
                 w_turn(turned_unit, 0)
                 w_turn(turned_unit, 1)
                 w_copy(turned_unit, 0)
+                if c == 1:
+                    f_regroup_first(0, 1)
                 w_copy(turned_unit, 1)
-            if c == 1:
-                f_quant(0, 1, 1)
+                if c == 1:
+                    f_regroup_first(1, 1)
+                    f_quant(0, 0, 1)
             if done_unit >= 0:
                 multiply(done_unit, 0)
             if c + 1 < TOTAL:
@@ -304,6 +304,8 @@ def tile_garnetlayer_t_kernel(tc, fi_v, d_av, out):
                 leave(done_unit, 1)
             if turned_unit >= 0 and c - 2 < pieces:
                 w_quant(turned_unit)
+            if c == 1:
+                f_quant(0, 1, 1)
             if 0 <= c - 2 < pieces:
                 f_quant(*piece(c - 2))
             if 0 <= c - 1 < pieces:

@@ -142,10 +142,10 @@ def tile_garnetlayer_t_kernel(tc, fi_v, d_av, out):
 
         def stage_a(g):
             sq = sqp.tile([P, 2, V], F32, name="sq")
-            for h in range(PASSES):
-                turned = dts[(g, h)][:].rearrange("q r p -> q (r p)").bitcast(BF16).rearrange(
-                    "q (x u f e) -> q e u x f", x=P, u=2, f=2, e=2)
-                for e in range(2):
+            for e in range(2):
+                for h in range(PASSES):
+                    turned = dts[(g, h)][:].rearrange("q r p -> q (r p)").bitcast(BF16).rearrange(
+                        "q (x u f e) -> q e u x f", x=P, u=2, f=2, e=2)
                     nc.scalar.activation(
                         out=sq[:, e, h * 512:(h + 1) * 512].rearrange("q (u x f) -> q u x f", u=2, x=P, f=2),
                         in_=turned[:, e],

@@ -244,8 +244,11 @@ def tile_garnetlayer_t_kernel(tc, fi_v, d_av, out):
 
         def store(g):
             b, c = divmod(g, UPG)
-            for e in range(2):
-                nc.sync.dma_start(out=o_view[b, c][:, e, :], in_=outs[g][:, e, :])
+            nc.sync.dma_start(out=o_view[b, c], in_=outs[g][:])
+
+        def store_half(g, e):
+            b, c = divmod(g, UPG)
+            nc.sync.dma_start(out=o_view[b, c][:, e, :], in_=outs[g][:, e, :])
 
         load_d_first(0, 0)
         load_d_first(0, 1)
@@ -269,11 +272,32 @@ def tile_garnetlayer_t_kernel(tc, fi_v, d_av, out):
             return 1 + j // PIECES, (j % PIECES) // NH, j % NH
 
         pieces = (GRAPHS - 1) * PIECES
+        warm = const.tile([P, NT], BF16)
+        nc.vector.memset(warm[:], 0.0)
+        idle = ps_acc.tile([P, NT], F32, name="acc")
+        for k in range(4):
+            nc.tensor.matmul(out=idle[:], lhsT=warm[:, 0:P], rhs=warm[:], start=True, stop=True)
         d_turn(0, [0, 1])
         for c in range(TOTAL):
             turned_unit = c - 1
             done_unit = c - 2
             stage_a(c)
+            if c == LAST:
+                w_scale(turned_unit)
+                w_turn(turned_unit, 0)
+                w_turn(turned_unit, 1)
+                w_copy(turned_unit, 0)
+                multiply(done_unit, 0)
+                multiply(done_unit, 1)
+                leave(done_unit, 0)
+                w_quant_half(turned_unit, 0)
+                leave(done_unit, 1)
+                w_copy(turned_unit, 1)
+                leave(done_unit, 2)
+                w_quant_half(turned_unit, 1)
+                leave(done_unit, 3)
+                store(c - 3)
+                continue
             if c == 0:
                 f_regroup_first(0, 0)
                 f_regroup_first(1, 0)
@@ -325,19 +349,21 @@ def tile_garnetlayer_t_kernel(tc, fi_v, d_av, out):
                     load_d(b, half)
 
         w_scale(LAST)
-        store(LAST - 2)
+        store_half(LAST - 2, 0)
+        store_half(LAST - 2, 1)
         w_turn(LAST, 0)
         multiply(LAST - 1, 0)
         w_turn(LAST, 1)
         multiply(LAST - 1, 1)
         w_copy(LAST, 0)
         exits(LAST - 1, 0)
+        store_half(LAST - 1, 0)
         w_copy(LAST, 1)
         w_quant_half(LAST, 0)
         multiply(LAST, 0)
         exits(LAST - 1, 1)
+        store_half(LAST - 1, 1)
         w_quant_half(LAST, 1)
         multiply(LAST, 1)
-        store(LAST - 1)
         exits(LAST, 0)
         exits(LAST, 1)

@@ -27,7 +27,7 @@ PIECES = PASSES * NH
 UNIT = 2 * P
 UPG = S // UNIT
 TOTAL = GRAPHS * UPG
-ACT_EXITS = {14: [0, 1, 2, 3], 15: [1, 3]}
+ACT_EXITS = {13: [3], 14: [0, 1, 2, 3], 15: [1, 3]}
 LAST = TOTAL - 1
 
 

@@ -318,7 +318,7 @@ def tile_garnetlayer_t_kernel(tc, fi_v, d_av, out):
             if done_unit >= 0:
                 multiply(done_unit, 0)
             if c + 1 < TOTAL:
-                d_turn(c + 1, [0])
+                d_turn(c + 1, [0, 1])
             if done_unit >= 0:
                 multiply(done_unit, 1)
                 leave(done_unit, 0)
@@ -336,8 +336,6 @@ def tile_garnetlayer_t_kernel(tc, fi_v, d_av, out):
                 f_regroup_pool(*piece(c - 1))
             if done_unit >= 0:
                 exits(done_unit, 1)
-            if c + 1 < TOTAL:
-                d_turn(c + 1, [1])
             if c >= 3:
                 store(c - 3)
             if c >= 1 and later:

from contextlib import ExitStack

import concourse.mybir as mybir
from concourse.masks import make_identity

FLOPS = 2 * 4 * 1024 * 1024 * 1024

F32 = mybir.dt.float32
BF16 = mybir.dt.bfloat16
U32 = mybir.dt.uint32
U8 = mybir.dt.uint8
FP8X4 = mybir.dt.float8_e4m3fn_x4
ACT = mybir.ActivationFunctionType
ALU = mybir.AluOpType

P = 128
PACK = 4
GRAPHS = 4
V = 1024
S = 1024
N = 1024
PASSES = V // (P * PACK)
ROWS = V // P
NT = 512
NH = N // NT
PIECES = PASSES * NH
UNIT = 2 * P
UPG = S // UNIT
TOTAL = GRAPHS * UPG
ACT_EXITS = {13: [3], 14: [0, 1, 2, 3], 15: [1, 3]}
LAST = TOTAL - 1


def tile_garnetlayer_t_kernel(tc, fi_v, d_av, out):
    nc = tc.nc
    d_view = d_av.rearrange("b (r p) s -> b p r s", p=P)
    f_view = fi_v.rearrange("b (h p j) n -> b h p j n", h=PASSES, p=P, j=PACK)
    o_view = out.rearrange("b (c q e n) -> b c q e n", c=UPG, q=P, e=2, n=N)

    with ExitStack() as ctx:
        const = ctx.enter_context(tc.tile_pool(name="const", bufs=1))
        rawd0 = ctx.enter_context(tc.tile_pool(name="rawd0", bufs=1))
        rawd = ctx.enter_context(tc.tile_pool(name="rawd", bufs=4))
        rawf = ctx.enter_context(tc.tile_pool(name="rawf", bufs=4))
        rawf0 = ctx.enter_context(tc.tile_pool(name="rawf0", bufs=PIECES))
        sqp = ctx.enter_context(tc.tile_pool(name="sqp", bufs=2))
        wtp = ctx.enter_context(tc.tile_pool(name="wtp", bufs=3))
        wgp = ctx.enter_context(tc.tile_pool(name="wgp", bufs=2))
        wq = ctx.enter_context(tc.tile_pool(name="wq", bufs=3))
        fg0p = ctx.enter_context(tc.tile_pool(name="fg0p", bufs=2))
        fgp = ctx.enter_context(tc.tile_pool(name="fgp", bufs=1))
        fq = ctx.enter_context(tc.tile_pool(name="fq", bufs=2))
        small = ctx.enter_context(tc.tile_pool(name="small", bufs=6))
        outp = ctx.enter_context(tc.tile_pool(name="outp", bufs=5))
        ps_d = ctx.enter_context(tc.psum_pool(name="ps_d", bufs=2))
        ps_w = ctx.enter_context(tc.psum_pool(name="ps_w", bufs=2))
        ps_acc = ctx.enter_context(tc.psum_pool(name="ps_acc", bufs=4))
        ctx.enter_context(tc.manual_schedule())

        zero = const.tile([P, 1], F32)
        nc.vector.memset(zero[:], 0.0)
        one = const.tile([P, 1], F32)
        nc.scalar.activation(out=one[:], in_=zero[:], func=ACT.Exp)

        ident = const.tile([P, P], F32)
        make_identity(nc, ident[:])

        d_raw = {}
        f_raw = {}
        f_first = {}
        f_codes = {}
        f_scales = {}
        fgs = {}
        dts = {}
        wts = {}
        bars = {}
        wps = {}
        wgs = {}
        codes = {}
        accs = {}
        outs = {}

        def load_d_first(c, h):
            piece = rawd0.tile([P, PACK, UNIT], BF16, name="d_first_%d_%d" % (c, h))
            nc.sync.dma_start(
                out=piece[:], in_=d_view[0][:, PACK * h:PACK * (h + 1), c * UNIT:(c + 1) * UNIT]
            )
            for r in range(PACK):
                d_raw[(c, PACK * h + r)] = piece[:, r, :]

        def load_d(b, half):
            piece = rawd.tile([P, ROWS, S // 2], BF16, name="d_half")
            nc.sync.dma_start(out=piece[:], in_=d_view[b][:, :, half * (S // 2):(half + 1) * (S // 2)])
            for c in range(2):
                for r in range(ROWS):
                    d_raw[(b * UPG + 2 * half + c, r)] = piece[:, r, c * UNIT:(c + 1) * UNIT]

        def load_f(b, h):
            f_raw[(b, h)] = rawf.tile([P, PACK, N], BF16, name="f_raw")
            nc.sync.dma_start(out=f_raw[(b, h)][:], in_=f_view[b, h])

        def load_f_piece(h, nh):
            f_first[(h, nh)] = rawf0.tile([P, PACK, NT], BF16, name="f_first")
            nc.sync.dma_start(out=f_first[(h, nh)][:], in_=f_view[0, h][:, :, nh * NT:(nh + 1) * NT])

        def f_regroup_first(h, nh):
            fg = fg0p.tile([P, NT, PACK], BF16, name="fg0", align_bytes=64)
            nc.vector.tensor_copy(
                out=fg[:].rearrange("p (c i) t -> p c t i", i=4),
                in_=f_first[(h, nh)][:].rearrange("p t (c i) -> p c t i", i=4),
            )
            fgs[(0, h, nh)] = fg

        def f_regroup_pool(b, h, nh):
            fg = fgp.tile([P, NT, PACK], BF16, name="fg", align_bytes=64)
            nc.gpsimd.tensor_scalar(
                out=fg[:],
                in0=f_raw[(b, h)][:, :, nh * NT:(nh + 1) * NT].rearrange("p t n -> p n t"),
                scalar1=1.0, scalar2=0.0, op0=ALU.mult, op1=ALU.add,
            )
            fgs[(b, h, nh)] = fg

        def f_quant(b, h, nh):
            if b not in f_codes:
                f_codes[b] = fq.tile([P, PASSES, N], U32, name="f_codes", align_bytes=64)
                f_scales[b] = fq.tile([P, PASSES, N], U8, name="f_scales", align_bytes=64)
            cols = slice(nh * NT, (nh + 1) * NT)
            nc.vector.quantize_mx(
                out=f_codes[b][:, h, cols].bitcast(FP8X4),
                scales=f_scales[b][:, h, cols],
                in_=fgs[(b, h, nh)][:].rearrange("p n t -> p (n t)"),
            )

        def d_turn(g, halves):
            for h in halves:
                dt = ps_d.tile([P, PACK, P], F32, name="dt")
                for r in range(PACK):
                    nc.tensor.transpose(
                        dt[:, r, :], d_raw[(g, PACK * h + r)].bitcast(F32), ident[:]
                    )
                dts[(g, h)] = dt

        def stage_a(g):
            sq = sqp.tile([P, 2, V], F32, name="sq")
            for e in range(2):
                for h in range(PASSES):
                    turned = dts[(g, h)][:].rearrange("q r p -> q (r p)").bitcast(BF16).rearrange(
                        "q (x u f e) -> q e u x f", x=P, u=2, f=2, e=2)
                    nc.scalar.activation(
                        out=sq[:, e, h * 512:(h + 1) * 512].rearrange("q (u x f) -> q u x f", u=2, x=P, f=2),
                        in_=turned[:, e],
                        func=ACT.Square,
                    )
            wt = wtp.tile([P, 2, V], BF16, name="wt")
            wsum = small.tile([P, 2], F32, name="wsum")
            for e in range(2):
                nc.scalar.activation(
                    out=wt[:, e, :], in_=sq[:, e, :], func=ACT.Exp, scale=-1.0, accum_out=wsum[:, e:e + 1]
                )
            wts[g] = wt
            bars[g] = [wsum, None]

        def w_scale(g):
            wbar = small.tile([P, 2], F32, name="wbar")
            nc.gpsimd.tensor_scalar(
                out=wbar[:], in0=bars[g][0][:], scalar1=2.0 ** -20, scalar2=0.0, op0=ALU.mult, op1=ALU.add
            )
            bars[g][1] = wbar

        def w_turn(g, e):
            wp = ps_w.tile([P, PACK, P], F32, name="wp")
            for k in range(PACK):
                nc.tensor.transpose(wp[:, k, :], wts[g][:, e, k * 256:(k + 1) * 256].bitcast(F32), ident[:])
            wps[(g, e)] = wp

        def w_copy(g, e):
            if g not in wgs:
                wgs[g] = wgp.tile([P, 2, PASSES, P, 2], F32, name="wg", align_bytes=64)
            nc.vector.tensor_copy(
                out=wgs[g][:, e], in_=wps[(g, e)][:].rearrange("p (h u) q -> p h q u", h=PASSES)
            )

        def w_quant(g):
            wc = wq.tile([P, 2 * PASSES * P], U32, name="wc", align_bytes=64)
            wl = wq.tile([P, 2 * PASSES * P], U8, name="wl", align_bytes=64)
            nc.vector.quantize_mx(
                out=wc[:].bitcast(FP8X4), scales=wl[:],
                in_=wgs[g][:].rearrange("p e h q u -> p (e h q u)").bitcast(BF16),
            )
            codes[g] = (wc, wl)

        def w_quant_half(g, e):
            if g not in codes:
                wc = wq.tile([P, 2 * PASSES * P], U32, name="wc", align_bytes=64)
                wl = wq.tile([P, 2 * PASSES * P], U8, name="wl", align_bytes=64)
                codes[g] = (wc, wl)
            wc, wl = codes[g]
            cols = slice(e * PASSES * P, (e + 1) * PASSES * P)
            nc.vector.quantize_mx(
                out=wc[:, cols].bitcast(FP8X4), scales=wl[:, cols],
                in_=wgs[g][:, e].rearrange("p h q u -> p (h q u)").bitcast(BF16),
            )

        def multiply(g, e):
            b = g // UPG
            wc, wl = codes[g]
            for nh in range(NH):
                cols = slice(nh * NT, (nh + 1) * NT)
                acc = ps_acc.tile([P, NT], F32, name="acc")
                for h in range(PASSES):
                    wcols = slice((e * PASSES + h) * P, (e * PASSES + h + 1) * P)
                    nc.tensor.matmul_mx(
                        out=acc[:],
                        lhsT=wc[:, wcols].bitcast(FP8X4),
                        lhsT_scale=wl[:, wcols],
                        rhs=f_codes[b][:, h, cols].bitcast(FP8X4),
                        rhs_scale=f_scales[b][:, h, cols],
                        start=(h == 0),
                        stop=(h == PASSES - 1),
                    )
                accs[(g, e * NH + nh)] = acc

        def exits(g, e):
            for nh in range(NH):
                leave(g, e * NH + nh)

        def leave(g, i):
            b, c = divmod(g, UPG)
            e, nh = divmod(i, NH)
            if g not in outs:
                outs[g] = outp.tile([P, 2, N], F32, name="o")
            if True:
                dst = outs[g][:, e, nh * NT:(nh + 1) * NT]
                if i in ACT_EXITS.get(g, []):
                    nc.scalar.activation(out=dst, in_=accs[(g, i)][:], func=ACT.Copy, scale=bars[g][1][:, e:e + 1])
                else:
                    nc.vector.tensor_scalar(
                        out=dst, in0=accs[(g, i)][:], scalar1=bars[g][0][:, e:e + 1], scalar2=2.0 ** -20,
                        op0=ALU.mult, op1=ALU.mult,
                    )
                if g == LAST:
                    cols = slice(nh * NT, (nh + 1) * NT)
                    nc.sync.dma_start(out=o_view[b, c][:, e, cols], in_=outs[g][:, e, cols])

        def store(g):
            b, c = divmod(g, UPG)
            nc.sync.dma_start(out=o_view[b, c], in_=outs[g][:])

        def store_half(g, e):
            b, c = divmod(g, UPG)
            nc.sync.dma_start(out=o_view[b, c][:, e, :], in_=outs[g][:, e, :])

        load_d_first(0, 0)
        load_d_first(0, 1)
        load_f_piece(0, 0)
        load_f_piece(1, 0)
        load_d_first(1, 0)
        load_d_first(1, 1)
        load_f_piece(0, 1)
        load_f_piece(1, 1)
        load_d_first(2, 0)
        load_d_first(2, 1)
        load_f(1, 0)
        load_d_first(3, 0)
        load_d_first(3, 1)
        load_d(1, 0)
        load_f(1, 1)
        later = [("d", 1, 1), ("f", 2, 0), ("d", 2, 0), ("f", 2, 1), ("d", 2, 1), ("f", 3, 0), ("d", 3, 0),
                 ("f", 3, 1), ("d", 3, 1)]

        def piece(j):
            return 1 + j // PIECES, (j % PIECES) // NH, j % NH

        pieces = (GRAPHS - 1) * PIECES
        warm = const.tile([P, NT], BF16)
        nc.vector.memset(warm[:], 0.0)
        idle = ps_acc.tile([P, NT], F32, name="acc")
        for k in range(4):
            nc.tensor.matmul(out=idle[:], lhsT=warm[:, 0:P], rhs=warm[:], start=True, stop=True)
        d_turn(0, [0, 1])
        for c in range(TOTAL):
            turned_unit = c - 1
            done_unit = c - 2
            stage_a(c)
            if c == LAST:
                w_scale(turned_unit)
                w_turn(turned_unit, 0)
                w_turn(turned_unit, 1)
                w_copy(turned_unit, 0)
                multiply(done_unit, 0)
                multiply(done_unit, 1)
                leave(done_unit, 0)
                w_quant_half(turned_unit, 0)
                leave(done_unit, 1)
                w_copy(turned_unit, 1)
                leave(done_unit, 2)
                w_quant_half(turned_unit, 1)
                leave(done_unit, 3)
                store(c - 3)
                continue
            if c == 0:
                f_regroup_first(0, 0)
                f_regroup_first(1, 0)
                f_quant(0, 0, 0)
                f_quant(0, 1, 0)
            if turned_unit >= 0:
                if ACT_EXITS.get(turned_unit):
                    w_scale(turned_unit)
                w_turn(turned_unit, 0)
                w_turn(turned_unit, 1)
                w_copy(turned_unit, 0)
                if c == 1:
                    f_regroup_first(0, 1)
                w_copy(turned_unit, 1)
                if c == 1:
                    f_regroup_first(1, 1)
                    f_quant(0, 0, 1)
            if done_unit >= 0:
                multiply(done_unit, 0)
            if c + 1 < TOTAL:
                d_turn(c + 1, [0, 1])
            if done_unit >= 0:
                multiply(done_unit, 1)
                leave(done_unit, 0)
            if c - 2 >= pieces:
                w_quant(turned_unit)
            if done_unit >= 0:
                leave(done_unit, 1)
            if turned_unit >= 0 and c - 2 < pieces:
                w_quant(turned_unit)
            if c == 1:
                f_quant(0, 1, 1)
            if 0 <= c - 2 < pieces:
                f_quant(*piece(c - 2))
            if 0 <= c - 1 < pieces:
                f_regroup_pool(*piece(c - 1))
            if done_unit >= 0:
                exits(done_unit, 1)
            if c >= 3:
                store(c - 3)
            if c >= 1 and later:
                kind, b, half = later[0]
                later = later[1:]
                if kind == "f":
                    load_f(b, half)
                else:
                    load_d(b, half)

        w_scale(LAST)
        store_half(LAST - 2, 0)
        store_half(LAST - 2, 1)
        w_turn(LAST, 0)
        multiply(LAST - 1, 0)
        w_turn(LAST, 1)
        multiply(LAST - 1, 1)
        w_copy(LAST, 0)
        exits(LAST - 1, 0)
        store_half(LAST - 1, 0)
        w_copy(LAST, 1)
        w_quant_half(LAST, 0)
        multiply(LAST, 0)
        exits(LAST - 1, 1)
        store_half(LAST - 1, 1)
        w_quant_half(LAST, 1)
        multiply(LAST, 1)
        exits(LAST, 0)
        exits(LAST, 1)
